import numpy as np
import ml_dtypes


def mxq(x, axis, fmt="e4m3"):
    dtype, down = {"e4m3": (ml_dtypes.float8_e4m3fn, 7), "e5m2": (ml_dtypes.float8_e5m2, 14)}[fmt]
    v = np.moveaxis(np.asarray(x, np.float32).astype(ml_dtypes.bfloat16).astype(np.float64), axis, -1)
    blocks = v.reshape(v.shape[:-1] + (-1, 32))
    amax = np.abs(blocks).max(-1, keepdims=True)
    byte = np.maximum(np.where(amax > 0, np.frexp(amax)[1] - 1 + 127, 0) - down, 1)
    scale = np.exp2(byte - 127.0)
    codes = (blocks / scale).astype(np.float32).astype(dtype).astype(np.float64)
    return np.moveaxis((codes * scale).reshape(v.shape), -1, axis)


WIDE = False


def mx_kscale(k):
    if not WIDE:
        return np.ones(k)
    levels = np.array([20, -20, 10, -10, 0])
    a = np.random.permutation(np.resize(levels, k // 512 * 4)).reshape(k // 512, 4)
    idx = np.arange(k)
    return np.exp2(a[idx // 512, idx % 128 // 32])


BF16 = ml_dtypes.bfloat16


def bf(x):
    return np.asarray(x, np.float32).astype(BF16)


def f64(x):
    return np.asarray(x).astype(np.float64)


B, S, IN, OUT, GROUP = 4, 256, 2048, 2048, 128
T = B * S
SCALE_RATIO = 1.4171
EPS = 1e-6


def softplus(v):
    return np.logaddexp(v, 0.0)


def sigmoid(v):
    return np.exp(-np.logaddexp(0.0, -v))


def setup_inputs():
    s = mx_kscale(T).reshape(B, S, 1)
    x = np.random.standard_normal((B, S, IN)) * s
    latent = np.random.standard_normal((OUT, IN)) / np.sqrt(IN)
    base_scale = np.abs(latent.reshape(OUT, IN // GROUP, GROUP)).mean(axis=-1) * SCALE_RATIO
    base_scale = base_scale * np.exp2(np.random.uniform(-1.0, 1.0, (OUT, IN // GROUP)))
    raw_scales = np.log(np.expm1(base_scale) + EPS)
    g = np.random.standard_normal((B, S, OUT)) * np.exp2(np.random.randint(-12, 1, (B, S, 1))) / s
    return {"x": bf(x), "weight_logits": bf(latent), "raw_scales": bf(raw_scales), "grad_out": bf(g)}


def reference(x, weight_logits, raw_scales, grad_out):
    xt = f64(x).reshape(T, IN)
    gt = f64(grad_out).reshape(T, OUT)
    gw = mxq(gt, 0, "e5m2").T @ mxq(xt, 0, "e4m3")
    q = np.where(f64(weight_logits) >= 0, 1.0, -1.0)
    gs = (gw * q).reshape(OUT, IN // GROUP, GROUP).sum(axis=-1)
    return gs * sigmoid(f64(raw_scales))

@@ -1,0 +1,181 @@
+from contextlib import ExitStack
+
+import concourse.mybir as mybir
+
+F32 = mybir.dt.float32
+BF16 = mybir.dt.bfloat16
+U32 = mybir.dt.uint32
+U8 = mybir.dt.uint8
+E4M3X4 = mybir.dt.float8_e4m3fn_x4
+E5M2X4 = mybir.dt.float8_e5m2_x4
+ALU = mybir.AluOpType
+ACT = mybir.ActivationFunctionType
+
+P = 128
+PACK = 4
+K_PASS = P * PACK
+TOKENS = 1024
+PASSES = TOKENS // K_PASS
+IN = 2048
+OUT = 2048
+GROUP = 128
+GROUPS = IN // GROUP
+O_TILES = OUT // P
+BANK = 512
+BANKS = IN // BANK
+GROUPS_PER_BANK = BANK // GROUP
+UNIT = 1024
+HALF = UNIT // 2
+RUN = 4
+STORE_TILES = 4
+STORES = O_TILES // STORE_TILES
+BY_SCALAR = STORE_TILES * GROUPS - GROUPS_PER_BANK
+LATE_UNITS_AFTER_TILE = 1
+
+FLOPS = 2 * TOKENS * IN * OUT
+
+
+def tile_groupedstelinear_kernel(tc, x, weight_logits, raw_scales, grad_out, out):
+    nc = tc.nc
+    x_rows = x.flatten_outer_dims()
+    g_rows = grad_out.flatten_outer_dims()
+    w_tiles = weight_logits.rearrange("(t p) i -> t p i", p=P)
+    rs_view = raw_scales.rearrange("(t p) k -> p t k", p=P)
+    out_view = out.rearrange("(t p) k -> p t k", p=P)
+
+    with ExitStack() as ctx:
+        keep = ctx.enter_context(tc.tile_pool(name="keep", bufs=1))
+        raws = ctx.enter_context(tc.tile_pool(name="raws", bufs=8))
+        groupeds = ctx.enter_context(tc.tile_pool(name="groupeds", bufs=6))
+        weights = ctx.enter_context(tc.tile_pool(name="weights", bufs=4))
+        signs = ctx.enter_context(tc.tile_pool(name="signs", bufs=3))
+        prods = ctx.enter_context(tc.tile_pool(name="prods", bufs=6))
+        stores = ctx.enter_context(tc.tile_pool(name="stores", bufs=2))
+        psum = ctx.enter_context(tc.psum_pool(name="psum", bufs=8))
+
+        x_codes = keep.tile([P, PASSES, IN], U32, align_bytes=64)
+        x_scales = keep.tile([P, PASSES, IN], U8, align_bytes=64)
+        g_codes = keep.tile([P, PASSES, OUT], U32, align_bytes=64)
+        g_scales = keep.tile([P, PASSES, OUT], U8, align_bytes=64)
+
+        warm_in = keep.tile([P, 1], F32)
+        warm_out = keep.tile([P, 1], F32)
+        nc.vector.memset(warm_in[:], 0.0)
+        nc.scalar.activation(out=warm_out[:], in_=warm_in[:], func=ACT.Sigmoid)
+
+        def regroup(engine_copy, raw, first):
+            grouped = groupeds.tile([P, HALF, PACK], BF16, align_bytes=64)
+            engine_copy(
+                out=grouped[:].rearrange("p (r i) j -> p r j i", i=RUN),
+                in_=raw[:, :, first : first + HALF].rearrange("p j (r i) -> p r j i", i=RUN),
+            )
+            return grouped
+
+        def quantise(grouped, codes, scales, fmt, c, first):
+            nc.vector.quantize_mx(
+                out=codes[:, c, first : first + HALF].bitcast(fmt),
+                scales=scales[:, c, first : first + HALF],
+                in_=grouped[:].rearrange("p w j -> p (w j)"),
+            )
+
+        def prepare(units):
+            scalars_half = None
+            for rows, codes, scales, fmt, c, h in units:
+                first = h * UNIT
+                raw = raws.tile([P, PACK, UNIT], BF16)
+                nc.sync.dma_start(
+                    out=raw[:],
+                    in_=rows[c * K_PASS : (c + 1) * K_PASS, first : first + UNIT].rearrange(
+                        "(p j) w -> p j w", j=PACK
+                    ),
+                )
+                by_vector = regroup(nc.vector.tensor_copy, raw, 0)
+                by_scalar = regroup(nc.scalar.copy, raw, HALF)
+                if scalars_half is not None:
+                    quantise(*scalars_half)
+                quantise(by_vector, codes, scales, fmt, c, first)
+                scalars_half = (by_scalar, codes, scales, fmt, c, first + HALF)
+            quantise(*scalars_half)
+
+        x_units = [(x_rows, x_codes, x_scales, E4M3X4, c, h) for c in range(PASSES) for h in range(IN // UNIT)]
+        g_units = [(g_rows, g_codes, g_scales, E5M2X4, c, h) for h in range(OUT // UNIT) for c in range(PASSES)]
+        prepare(x_units + g_units[:PASSES])
+
+        rs_sb = keep.tile([P, O_TILES, GROUPS], BF16)
+        sig = keep.tile([P, O_TILES, GROUPS], F32)
+        sums = keep.tile([P, O_TILES * GROUPS], F32)
+        sums_v = keep.tile([P, STORES, GROUPS_PER_BANK], F32)
+
+        for t in range(O_TILES):
+            o_cols = slice(t * P, (t + 1) * P)
+            last_of_store = (t + 1) % STORE_TILES == 0
+            w_sb = weights.tile([P, IN], BF16)
+            nc.sync.dma_start(out=w_sb[:], in_=w_tiles[t])
+            half_sign = signs.tile([P, IN], BF16)
+            nc.vector.tensor_scalar(
+                out=half_sign[:], in0=w_sb[:], scalar1=0.0, scalar2=0.5, op0=ALU.is_ge, op1=ALU.subtract
+            )
+            for b in range(BANKS):
+                i_cols = slice(b * BANK, (b + 1) * BANK)
+                acc = psum.tile([P, BANK], F32)
+                for c in range(PASSES):
+                    nc.tensor.matmul_mx(
+                        out=acc[:],
+                        lhsT=g_codes[:, c, o_cols].bitcast(E5M2X4),
+                        lhsT_scale=g_scales[:, c, o_cols],
+                        rhs=x_codes[:, c, i_cols].bitcast(E4M3X4),
+                        rhs_scale=x_scales[:, c, i_cols],
+                        start=(c == 0),
+                        stop=(c == PASSES - 1),
+                    )
+                prod = prods.tile([P, BANK], F32)
+                if last_of_store and b == BANKS - 1:
+                    for q in range(GROUPS_PER_BANK):
+                        nc.vector.scalar_tensor_tensor(
+                            out=prod[:, q * GROUP : (q + 1) * GROUP],
+                            in0=acc[:, q * GROUP : (q + 1) * GROUP],
+                            scalar=1.0,
+                            in1=half_sign[:, b * BANK + q * GROUP : b * BANK + (q + 1) * GROUP],
+                            op0=ALU.mult,
+                            op1=ALU.mult,
+                            accum_out=sums_v[:, t // STORE_TILES, q : q + 1],
+                        )
+                else:
+                    nc.vector.tensor_tensor(out=prod[:], in0=acc[:], in1=half_sign[:, i_cols], op=ALU.mult)
+                    for q in range(GROUPS_PER_BANK):
+                        k = t * GROUPS + b * GROUPS_PER_BANK + q
+                        group_cols = slice(q * GROUP, (q + 1) * GROUP)
+                        nc.scalar.activation(
+                            out=prod[:, group_cols],
+                            in_=prod[:, group_cols],
+                            func=ACT.Copy,
+                            accum_out=sums[:, k : k + 1],
+                        )
+            if t == LATE_UNITS_AFTER_TILE:
+                prepare(g_units[PASSES:])
+                nc.sync.dma_start(out=rs_sb[:], in_=rs_view)
+                nc.scalar.activation(out=sig[:], in_=rs_sb[:], func=ACT.Sigmoid)
+            if last_of_store:
+                s = t // STORE_TILES
+                done = slice(s * STORE_TILES, (s + 1) * STORE_TILES)
+                first = s * STORE_TILES * GROUPS
+                result = stores.tile([P, STORE_TILES, GROUPS], F32)
+                result_flat = result[:].rearrange("p t k -> p (t k)")
+                sig_flat = sig[:, done, :].rearrange("p t k -> p (t k)")
+                nc.vector.scalar_tensor_tensor(
+                    out=result_flat[:, :BY_SCALAR],
+                    in0=sums[:, first : first + BY_SCALAR],
+                    scalar=2.0,
+                    in1=sig_flat[:, :BY_SCALAR],
+                    op0=ALU.mult,
+                    op1=ALU.mult,
+                )
+                nc.vector.scalar_tensor_tensor(
+                    out=result_flat[:, BY_SCALAR:],
+                    in0=sums_v[:, s, :],
+                    scalar=2.0,
+                    in1=sig_flat[:, BY_SCALAR:],
+                    op0=ALU.mult,
+                    op1=ALU.mult,
+                )
+                nc.sync.dma_start(out=out_view[:, done, :], in_=result[:])

@@ -28,8 +28,8 @@ UNIT = 1024
 HALF = UNIT // 2
 RUN = 4
 STORE_TILES = 4
-STORES = O_TILES // STORE_TILES
-BY_SCALAR = STORE_TILES * GROUPS - GROUPS_PER_BANK
+VECTOR_EVERY = 2
+BANKS_BY_VECTOR = 2
 LATE_UNITS_AFTER_TILE = 1
 
 FLOPS = 2 * TOKENS * IN * OUT
@@ -49,7 +49,7 @@ def tile_groupedstelinear_kernel(tc, x, weight_logits, raw_scales, grad_out, out
         groupeds = ctx.enter_context(tc.tile_pool(name="groupeds", bufs=6))
         weights = ctx.enter_context(tc.tile_pool(name="weights", bufs=4))
         signs = ctx.enter_context(tc.tile_pool(name="signs", bufs=3))
-        prods = ctx.enter_context(tc.tile_pool(name="prods", bufs=6))
+        prods = ctx.enter_context(tc.tile_pool(name="prods", bufs=10))
         stores = ctx.enter_context(tc.tile_pool(name="stores", bufs=2))
         psum = ctx.enter_context(tc.psum_pool(name="psum", bufs=8))
 
@@ -103,12 +103,11 @@ def tile_groupedstelinear_kernel(tc, x, weight_logits, raw_scales, grad_out, out
 
         rs_sb = keep.tile([P, O_TILES, GROUPS], BF16)
         sig = keep.tile([P, O_TILES, GROUPS], F32)
-        sums = keep.tile([P, O_TILES * GROUPS], F32)
-        sums_v = keep.tile([P, STORES, GROUPS_PER_BANK], F32)
+        sums = keep.tile([P, O_TILES, GROUPS], F32)
 
         for t in range(O_TILES):
             o_cols = slice(t * P, (t + 1) * P)
-            last_of_store = (t + 1) % STORE_TILES == 0
+            shared_tile = (t + 1) % VECTOR_EVERY == 0
             w_sb = weights.tile([P, IN], BF16)
             nc.sync.dma_start(out=w_sb[:], in_=w_tiles[t])
             half_sign = signs.tile([P, IN], BF16)
@@ -129,53 +128,37 @@ def tile_groupedstelinear_kernel(tc, x, weight_logits, raw_scales, grad_out, out
                         stop=(c == PASSES - 1),
                     )
                 prod = prods.tile([P, BANK], F32)
-                if last_of_store and b == BANKS - 1:
+                if shared_tile and b >= BANKS - BANKS_BY_VECTOR:
                     for q in range(GROUPS_PER_BANK):
+                        k = b * GROUPS_PER_BANK + q
                         nc.vector.scalar_tensor_tensor(
                             out=prod[:, q * GROUP : (q + 1) * GROUP],
                             in0=acc[:, q * GROUP : (q + 1) * GROUP],
                             scalar=1.0,
-                            in1=half_sign[:, b * BANK + q * GROUP : b * BANK + (q + 1) * GROUP],
+                            in1=half_sign[:, k * GROUP : (k + 1) * GROUP],
                             op0=ALU.mult,
                             op1=ALU.mult,
-                            accum_out=sums_v[:, t // STORE_TILES, q : q + 1],
+                            accum_out=sums[:, t, k : k + 1],
                         )
                 else:
                     nc.vector.tensor_tensor(out=prod[:], in0=acc[:], in1=half_sign[:, i_cols], op=ALU.mult)
                     for q in range(GROUPS_PER_BANK):
-                        k = t * GROUPS + b * GROUPS_PER_BANK + q
+                        k = b * GROUPS_PER_BANK + q
                         group_cols = slice(q * GROUP, (q + 1) * GROUP)
                         nc.scalar.activation(
                             out=prod[:, group_cols],
                             in_=prod[:, group_cols],
                             func=ACT.Copy,
-                            accum_out=sums[:, k : k + 1],
+                            accum_out=sums[:, t, k : k + 1],
                         )
             if t == LATE_UNITS_AFTER_TILE:
                 prepare(g_units[PASSES:])
                 nc.sync.dma_start(out=rs_sb[:], in_=rs_view)
                 nc.scalar.activation(out=sig[:], in_=rs_sb[:], func=ACT.Sigmoid)
-            if last_of_store:
-                s = t // STORE_TILES
-                done = slice(s * STORE_TILES, (s + 1) * STORE_TILES)
-                first = s * STORE_TILES * GROUPS
+            if (t + 1) % STORE_TILES == 0:
+                done = slice(t + 1 - STORE_TILES, t + 1)
                 result = stores.tile([P, STORE_TILES, GROUPS], F32)
-                result_flat = result[:].rearrange("p t k -> p (t k)")
-                sig_flat = sig[:, done, :].rearrange("p t k -> p (t k)")
                 nc.vector.scalar_tensor_tensor(
-                    out=result_flat[:, :BY_SCALAR],
-                    in0=sums[:, first : first + BY_SCALAR],
-                    scalar=2.0,
-                    in1=sig_flat[:, :BY_SCALAR],
-                    op0=ALU.mult,
-                    op1=ALU.mult,
-                )
-                nc.vector.scalar_tensor_tensor(
-                    out=result_flat[:, BY_SCALAR:],
-                    in0=sums_v[:, s, :],
-                    scalar=2.0,
-                    in1=sig_flat[:, BY_SCALAR:],
-                    op0=ALU.mult,
-                    op1=ALU.mult,
+                    out=result[:], in0=sums[:, done, :], scalar=2.0, in1=sig[:, done, :], op0=ALU.mult, op1=ALU.mult
                 )
                 nc.sync.dma_start(out=out_view[:, done, :], in_=result[:])

@@ -28,7 +28,7 @@ UNIT = 1024
 HALF = UNIT // 2
 RUN = 4
 STORE_TILES = 4
-VECTOR_EVERY = 2
+VECTOR_EVERY = 8
 BANKS_BY_VECTOR = 2
 LATE_UNITS_AFTER_TILE = 1
 

@@ -1,6 +1,7 @@
 from contextlib import ExitStack
 
 import concourse.mybir as mybir
+from concourse.masks import make_identity
 
 F32 = mybir.dt.float32
 BF16 = mybir.dt.bfloat16
@@ -30,6 +31,10 @@ RUN = 4
 STORE_TILES = 4
 VECTOR_EVERY = 8
 BANKS_BY_VECTOR = 2
+TENSOR_EVERY = 3
+TENSOR_LAG = 2
+SLICES = IN // P
+KEPT = GROUP // SLICES
 LATE_UNITS_AFTER_TILE = 1
 
 FLOPS = 2 * TOKENS * IN * OUT
@@ -51,7 +56,10 @@ def tile_groupedstelinear_kernel(tc, x, weight_logits, raw_scales, grad_out, out
         signs = ctx.enter_context(tc.tile_pool(name="signs", bufs=3))
         prods = ctx.enter_context(tc.tile_pool(name="prods", bufs=10))
         stores = ctx.enter_context(tc.tile_pool(name="stores", bufs=2))
-        psum = ctx.enter_context(tc.psum_pool(name="psum", bufs=8))
+        sliced = ctx.enter_context(tc.tile_pool(name="sliced", bufs=2))
+        turned = ctx.enter_context(tc.tile_pool(name="turned", bufs=2))
+        psum = ctx.enter_context(tc.psum_pool(name="psum", bufs=7))
+        psum_fold = ctx.enter_context(tc.psum_pool(name="psum_fold", bufs=1))
 
         x_codes = keep.tile([P, PASSES, IN], U32, align_bytes=64)
         x_scales = keep.tile([P, PASSES, IN], U8, align_bytes=64)
@@ -62,6 +70,13 @@ def tile_groupedstelinear_kernel(tc, x, weight_logits, raw_scales, grad_out, out
         warm_out = keep.tile([P, 1], F32)
         nc.vector.memset(warm_in[:], 0.0)
         nc.scalar.activation(out=warm_out[:], in_=warm_in[:], func=ACT.Sigmoid)
+
+        ident = keep.tile([P, P], F32)
+        make_identity(nc, ident[:])
+        chooser = keep.tile([P, GROUPS], F32)
+        nc.vector.tensor_reduce(
+            out=chooser[:], in_=ident[:].rearrange("p (k u) -> p k u", u=KEPT), axis=mybir.AxisListType.X, op=ALU.add
+        )
 
         def regroup(engine_copy, raw, first):
             grouped = groupeds.tile([P, HALF, PACK], BF16, align_bytes=64)
@@ -78,7 +93,7 @@ def tile_groupedstelinear_kernel(tc, x, weight_logits, raw_scales, grad_out, out
                 in_=grouped[:].rearrange("p w j -> p (w j)"),
             )
 
-        def prepare(units):
+        def prepare(units, first_copy):
             scalars_half = None
             for rows, codes, scales, fmt, c, h in units:
                 first = h * UNIT
@@ -89,7 +104,7 @@ def tile_groupedstelinear_kernel(tc, x, weight_logits, raw_scales, grad_out, out
                         "(p j) w -> p j w", j=PACK
                     ),
                 )
-                by_vector = regroup(nc.vector.tensor_copy, raw, 0)
+                by_vector = regroup(first_copy, raw, 0)
                 by_scalar = regroup(nc.scalar.copy, raw, HALF)
                 if scalars_half is not None:
                     quantise(*scalars_half)
@@ -99,17 +114,57 @@ def tile_groupedstelinear_kernel(tc, x, weight_logits, raw_scales, grad_out, out
 
         x_units = [(x_rows, x_codes, x_scales, E4M3X4, c, h) for c in range(PASSES) for h in range(IN // UNIT)]
         g_units = [(g_rows, g_codes, g_scales, E5M2X4, c, h) for h in range(OUT // UNIT) for c in range(PASSES)]
-        prepare(x_units + g_units[:PASSES])
+        prepare(x_units + g_units[:PASSES], nc.vector.tensor_copy)
 
         rs_sb = keep.tile([P, O_TILES, GROUPS], BF16)
         sig = keep.tile([P, O_TILES, GROUPS], F32)
         sums = keep.tile([P, O_TILES, GROUPS], F32)
 
+        def sum_by_tensor(t, slices):
+            fold = psum_fold.tile([P, BANK], F32)
+            for j in range(SLICES):
+                nc.tensor.matmul(
+                    out=fold[:, :P],
+                    lhsT=slices[:, j, :],
+                    rhs=ident[:],
+                    is_transpose=True,
+                    start=(j == 0),
+                    stop=(j == SLICES - 1),
+                )
+            fold_sb = turned.tile([P, P], F32)
+            nc.scalar.copy(out=fold_sb[:], in_=fold[:, :P])
+            group_sums = fold[:, P : P + GROUPS]
+            nc.tensor.matmul(out=group_sums, lhsT=fold_sb[:], rhs=chooser[:], start=True, stop=True)
+            nc.scalar.copy(out=sums[:, t, :], in_=group_sums)
+
+        def store(end):
+            done = slice(end - STORE_TILES, end)
+            result = stores.tile([P, STORE_TILES, GROUPS], F32)
+            nc.vector.scalar_tensor_tensor(
+                out=result[:], in0=sums[:, done, :], scalar=2.0, in1=sig[:, done, :], op0=ALU.mult, op1=ALU.mult
+            )
+            nc.sync.dma_start(out=out_view[:, done, :], in_=result[:])
+
+        late_raws = []
+        late_halves = [(c, UNIT + h * HALF) for h in range(UNIT // HALF) for c in range(PASSES)]
+        late_grouped = []
+        waiting = []
         for t in range(O_TILES):
             o_cols = slice(t * P, (t + 1) * P)
-            shared_tile = (t + 1) % VECTOR_EVERY == 0
+            shared_tile = t == O_TILES - 1
+            by_tensor = t % TENSOR_EVERY == 1
+            if by_tensor:
+                slices = sliced.tile([P, SLICES, P], F32)
             w_sb = weights.tile([P, IN], BF16)
             nc.sync.dma_start(out=w_sb[:], in_=w_tiles[t])
+            if t == LATE_UNITS_AFTER_TILE:
+                for c in range(PASSES):
+                    late_raw = raws.tile([P, PACK, UNIT], BF16, name="raw")
+                    nc.sync.dma_start(
+                        out=late_raw[:],
+                        in_=g_rows[c * K_PASS : (c + 1) * K_PASS, UNIT : 2 * UNIT].rearrange("(p j) w -> p j w", j=PACK),
+                    )
+                    late_raws.append(late_raw)
             half_sign = signs.tile([P, IN], BF16)
             nc.vector.tensor_scalar(
                 out=half_sign[:], in0=w_sb[:], scalar1=0.0, scalar2=0.5, op0=ALU.is_ge, op1=ALU.subtract
@@ -127,6 +182,15 @@ def tile_groupedstelinear_kernel(tc, x, weight_logits, raw_scales, grad_out, out
                         start=(c == 0),
                         stop=(c == PASSES - 1),
                     )
+                if by_tensor:
+                    places = slice(b * GROUPS_PER_BANK * KEPT, (b + 1) * GROUPS_PER_BANK * KEPT)
+                    nc.vector.tensor_tensor(
+                        out=slices[:, :, places].rearrange("p j (k u) -> p j k u", u=KEPT),
+                        in0=acc[:].rearrange("p (k j u) -> p j k u", j=SLICES, u=KEPT),
+                        in1=half_sign[:, i_cols].rearrange("p (k j u) -> p j k u", j=SLICES, u=KEPT),
+                        op=ALU.mult,
+                    )
+                    continue
                 prod = prods.tile([P, BANK], F32)
                 if shared_tile and b >= BANKS - BANKS_BY_VECTOR:
                     for q in range(GROUPS_PER_BANK):
@@ -151,14 +215,20 @@ def tile_groupedstelinear_kernel(tc, x, weight_logits, raw_scales, grad_out, out
                             func=ACT.Copy,
                             accum_out=sums[:, t, k : k + 1],
                         )
+            if waiting and waiting[0][0] <= t - TENSOR_LAG:
+                sum_by_tensor(*waiting.pop())
+            if by_tensor:
+                waiting.append((t, slices))
+            if late_grouped:
+                quantise(*late_grouped.pop())
+            if by_tensor and late_halves:
+                c, first = late_halves.pop(0)
+                late_grouped.append(
+                    (regroup(nc.scalar.copy, late_raws[c], first - UNIT), g_codes, g_scales, E5M2X4, c, first)
+                )
             if t == LATE_UNITS_AFTER_TILE:
-                prepare(g_units[PASSES:])
                 nc.sync.dma_start(out=rs_sb[:], in_=rs_view)
                 nc.scalar.activation(out=sig[:], in_=rs_sb[:], func=ACT.Sigmoid)
-            if (t + 1) % STORE_TILES == 0:
-                done = slice(t + 1 - STORE_TILES, t + 1)
-                result = stores.tile([P, STORE_TILES, GROUPS], F32)
-                nc.vector.scalar_tensor_tensor(
-                    out=result[:], in0=sums[:, done, :], scalar=2.0, in1=sig[:, done, :], op0=ALU.mult, op1=ALU.mult
-                )
-                nc.sync.dma_start(out=out_view[:, done, :], in_=result[:])
+            if t % STORE_TILES == 1 and t > 1:
+                store(t - 1)
+        store(O_TILES)

@@ -31,6 +31,9 @@ RUN = 4
 STORE_TILES = 4
 VECTOR_EVERY = 8
 BANKS_BY_VECTOR = 2
+EARLY_TILES = 4
+QUANTISE_LAG = 2
+STORE_LAG = 3
 TENSOR_EVERY = 3
 TENSOR_LAG = 2
 SLICES = IN // P
@@ -53,8 +56,8 @@ def tile_groupedstelinear_kernel(tc, x, weight_logits, raw_scales, grad_out, out
         raws = ctx.enter_context(tc.tile_pool(name="raws", bufs=8))
         groupeds = ctx.enter_context(tc.tile_pool(name="groupeds", bufs=6))
         weights = ctx.enter_context(tc.tile_pool(name="weights", bufs=4))
-        signs = ctx.enter_context(tc.tile_pool(name="signs", bufs=3))
-        prods = ctx.enter_context(tc.tile_pool(name="prods", bufs=10))
+        signs = ctx.enter_context(tc.tile_pool(name="signs", bufs=6))
+        prods = ctx.enter_context(tc.tile_pool(name="prods", bufs=12))
         stores = ctx.enter_context(tc.tile_pool(name="stores", bufs=2))
         sliced = ctx.enter_context(tc.tile_pool(name="sliced", bufs=2))
         turned = ctx.enter_context(tc.tile_pool(name="turned", bufs=2))
@@ -112,9 +115,9 @@ def tile_groupedstelinear_kernel(tc, x, weight_logits, raw_scales, grad_out, out
                 scalars_half = (by_scalar, codes, scales, fmt, c, first + HALF)
             quantise(*scalars_half)
 
-        x_units = [(x_rows, x_codes, x_scales, E4M3X4, c, h) for c in range(PASSES) for h in range(IN // UNIT)]
+        x_units = [(x_rows, x_codes, x_scales, E4M3X4, c, h) for h in range(IN // UNIT) for c in range(PASSES)]
         g_units = [(g_rows, g_codes, g_scales, E5M2X4, c, h) for h in range(OUT // UNIT) for c in range(PASSES)]
-        prepare(x_units + g_units[:PASSES], nc.vector.tensor_copy)
+        prepare(x_units[:PASSES] + g_units[:PASSES] + x_units[PASSES:], nc.vector.tensor_copy)
 
         rs_sb = keep.tile([P, O_TILES, GROUPS], BF16)
         sig = keep.tile([P, O_TILES, GROUPS], F32)
@@ -149,15 +152,16 @@ def tile_groupedstelinear_kernel(tc, x, weight_logits, raw_scales, grad_out, out
         late_halves = [(c, UNIT + h * HALF) for h in range(UNIT // HALF) for c in range(PASSES)]
         late_grouped = []
         waiting = []
-        for t in range(O_TILES):
-            o_cols = slice(t * P, (t + 1) * P)
-            shared_tile = t == O_TILES - 1
-            by_tensor = t % TENSOR_EVERY == 1
-            if by_tensor:
+        half_signs = {}
+        slices_of = {}
+
+        def start_tile(t):
+            if t % TENSOR_EVERY == 1:
                 slices = sliced.tile([P, SLICES, P], F32)
+                slices_of[t] = slices
             w_sb = weights.tile([P, IN], BF16)
             nc.sync.dma_start(out=w_sb[:], in_=w_tiles[t])
-            if t == LATE_UNITS_AFTER_TILE:
+            if t == EARLY_TILES - 1:
                 for c in range(PASSES):
                     late_raw = raws.tile([P, PACK, UNIT], BF16, name="raw")
                     nc.sync.dma_start(
@@ -169,66 +173,86 @@ def tile_groupedstelinear_kernel(tc, x, weight_logits, raw_scales, grad_out, out
             nc.vector.tensor_scalar(
                 out=half_sign[:], in0=w_sb[:], scalar1=0.0, scalar2=0.5, op0=ALU.is_ge, op1=ALU.subtract
             )
-            for b in range(BANKS):
-                i_cols = slice(b * BANK, (b + 1) * BANK)
-                acc = psum.tile([P, BANK], F32)
-                for c in range(PASSES):
-                    nc.tensor.matmul_mx(
-                        out=acc[:],
-                        lhsT=g_codes[:, c, o_cols].bitcast(E5M2X4),
-                        lhsT_scale=g_scales[:, c, o_cols],
-                        rhs=x_codes[:, c, i_cols].bitcast(E4M3X4),
-                        rhs_scale=x_scales[:, c, i_cols],
-                        start=(c == 0),
-                        stop=(c == PASSES - 1),
+            half_signs[t] = half_sign
+
+        def bank(t, b):
+            o_cols = slice(t * P, (t + 1) * P)
+            i_cols = slice(b * BANK, (b + 1) * BANK)
+            half_sign = half_signs[t]
+            acc = psum.tile([P, BANK], F32)
+            for c in range(PASSES):
+                nc.tensor.matmul_mx(
+                    out=acc[:],
+                    lhsT=g_codes[:, c, o_cols].bitcast(E5M2X4),
+                    lhsT_scale=g_scales[:, c, o_cols],
+                    rhs=x_codes[:, c, i_cols].bitcast(E4M3X4),
+                    rhs_scale=x_scales[:, c, i_cols],
+                    start=(c == 0),
+                    stop=(c == PASSES - 1),
+                )
+            if t in slices_of:
+                places = slice(b * GROUPS_PER_BANK * KEPT, (b + 1) * GROUPS_PER_BANK * KEPT)
+                nc.vector.tensor_tensor(
+                    out=slices_of[t][:, :, places].rearrange("p j (k u) -> p j k u", u=KEPT),
+                    in0=acc[:].rearrange("p (k j u) -> p j k u", j=SLICES, u=KEPT),
+                    in1=half_sign[:, i_cols].rearrange("p (k j u) -> p j k u", j=SLICES, u=KEPT),
+                    op=ALU.mult,
+                )
+                return
+            prod = prods.tile([P, BANK], F32)
+            if t == O_TILES - 1 and b >= BANKS - BANKS_BY_VECTOR:
+                for q in range(GROUPS_PER_BANK):
+                    k = b * GROUPS_PER_BANK + q
+                    nc.vector.scalar_tensor_tensor(
+                        out=prod[:, q * GROUP : (q + 1) * GROUP],
+                        in0=acc[:, q * GROUP : (q + 1) * GROUP],
+                        scalar=1.0,
+                        in1=half_sign[:, k * GROUP : (k + 1) * GROUP],
+                        op0=ALU.mult,
+                        op1=ALU.mult,
+                        accum_out=sums[:, t, k : k + 1],
                     )
-                if by_tensor:
-                    places = slice(b * GROUPS_PER_BANK * KEPT, (b + 1) * GROUPS_PER_BANK * KEPT)
-                    nc.vector.tensor_tensor(
-                        out=slices[:, :, places].rearrange("p j (k u) -> p j k u", u=KEPT),
-                        in0=acc[:].rearrange("p (k j u) -> p j k u", j=SLICES, u=KEPT),
-                        in1=half_sign[:, i_cols].rearrange("p (k j u) -> p j k u", j=SLICES, u=KEPT),
-                        op=ALU.mult,
-                    )
-                    continue
-                prod = prods.tile([P, BANK], F32)
-                if shared_tile and b >= BANKS - BANKS_BY_VECTOR:
-                    for q in range(GROUPS_PER_BANK):
-                        k = b * GROUPS_PER_BANK + q
-                        nc.vector.scalar_tensor_tensor(
-                            out=prod[:, q * GROUP : (q + 1) * GROUP],
-                            in0=acc[:, q * GROUP : (q + 1) * GROUP],
-                            scalar=1.0,
-                            in1=half_sign[:, k * GROUP : (k + 1) * GROUP],
-                            op0=ALU.mult,
-                            op1=ALU.mult,
-                            accum_out=sums[:, t, k : k + 1],
-                        )
-                else:
-                    nc.vector.tensor_tensor(out=prod[:], in0=acc[:], in1=half_sign[:, i_cols], op=ALU.mult)
-                    for q in range(GROUPS_PER_BANK):
-                        k = b * GROUPS_PER_BANK + q
-                        group_cols = slice(q * GROUP, (q + 1) * GROUP)
-                        nc.scalar.activation(
-                            out=prod[:, group_cols],
-                            in_=prod[:, group_cols],
-                            func=ACT.Copy,
-                            accum_out=sums[:, t, k : k + 1],
-                        )
+                return
+            nc.vector.tensor_tensor(out=prod[:], in0=acc[:], in1=half_sign[:, i_cols], op=ALU.mult)
+            for q in range(GROUPS_PER_BANK):
+                k = b * GROUPS_PER_BANK + q
+                group_cols = slice(q * GROUP, (q + 1) * GROUP)
+                nc.scalar.activation(
+                    out=prod[:, group_cols], in_=prod[:, group_cols], func=ACT.Copy, accum_out=sums[:, t, k : k + 1]
+                )
+
+        def end_tile(t):
             if waiting and waiting[0][0] <= t - TENSOR_LAG:
                 sum_by_tensor(*waiting.pop())
-            if by_tensor:
-                waiting.append((t, slices))
-            if late_grouped:
-                quantise(*late_grouped.pop())
-            if by_tensor and late_halves:
+            if t in slices_of:
+                waiting.append((t, slices_of[t]))
+            if late_grouped and late_grouped[0][0] <= t - QUANTISE_LAG:
+                quantise(*late_grouped.pop(0)[1])
+            if t in slices_of and late_halves:
                 c, first = late_halves.pop(0)
                 late_grouped.append(
-                    (regroup(nc.scalar.copy, late_raws[c], first - UNIT), g_codes, g_scales, E5M2X4, c, first)
+                    (
+                        min(t, O_TILES - 7),
+                        (regroup(nc.scalar.copy, late_raws[c], first - UNIT), g_codes, g_scales, E5M2X4, c, first),
+                    )
                 )
             if t == LATE_UNITS_AFTER_TILE:
                 nc.sync.dma_start(out=rs_sb[:], in_=rs_view)
                 nc.scalar.activation(out=sig[:], in_=rs_sb[:], func=ACT.Sigmoid)
-            if t % STORE_TILES == 1 and t > 1:
-                store(t - 1)
+            if t % STORE_TILES == STORE_LAG and t > STORE_TILES:
+                store(t - STORE_LAG)
+
+        for t in range(EARLY_TILES):
+            start_tile(t)
+            for b in range(BANKS // 2):
+                bank(t, b)
+        for t in range(EARLY_TILES):
+            for b in range(BANKS // 2, BANKS):
+                bank(t, b)
+            end_tile(t)
+        for t in range(EARLY_TILES, O_TILES):
+            start_tile(t)
+            for b in range(BANKS):
+                bank(t, b)
+            end_tile(t)
         store(O_TILES)

from contextlib import ExitStack

import concourse.mybir as mybir
from concourse.masks import make_identity

F32 = mybir.dt.float32
BF16 = mybir.dt.bfloat16
U32 = mybir.dt.uint32
U8 = mybir.dt.uint8
E4M3X4 = mybir.dt.float8_e4m3fn_x4
E5M2X4 = mybir.dt.float8_e5m2_x4
ALU = mybir.AluOpType
ACT = mybir.ActivationFunctionType

P = 128
PACK = 4
K_PASS = P * PACK
TOKENS = 1024
PASSES = TOKENS // K_PASS
IN = 2048
OUT = 2048
GROUP = 128
GROUPS = IN // GROUP
O_TILES = OUT // P
BANK = 512
BANKS = IN // BANK
GROUPS_PER_BANK = BANK // GROUP
UNIT = 1024
HALF = UNIT // 2
RUN = 4
STORE_TILES = 4
VECTOR_EVERY = 8
BANKS_BY_VECTOR = 2
EARLY_TILES = 4
QUANTISE_LAG = 2
STORE_LAG = 3
TENSOR_EVERY = 3
TENSOR_LAG = 2
SLICES = IN // P
KEPT = GROUP // SLICES
LATE_UNITS_AFTER_TILE = 1

FLOPS = 2 * TOKENS * IN * OUT


def tile_groupedstelinear_kernel(tc, x, weight_logits, raw_scales, grad_out, out):
    nc = tc.nc
    x_rows = x.flatten_outer_dims()
    g_rows = grad_out.flatten_outer_dims()
    w_tiles = weight_logits.rearrange("(t p) i -> t p i", p=P)
    rs_view = raw_scales.rearrange("(t p) k -> p t k", p=P)
    out_view = out.rearrange("(t p) k -> p t k", p=P)

    with ExitStack() as ctx:
        keep = ctx.enter_context(tc.tile_pool(name="keep", bufs=1))
        raws = ctx.enter_context(tc.tile_pool(name="raws", bufs=8))
        groupeds = ctx.enter_context(tc.tile_pool(name="groupeds", bufs=6))
        weights = ctx.enter_context(tc.tile_pool(name="weights", bufs=4))
        signs = ctx.enter_context(tc.tile_pool(name="signs", bufs=6))
        prods = ctx.enter_context(tc.tile_pool(name="prods", bufs=12))
        stores = ctx.enter_context(tc.tile_pool(name="stores", bufs=2))
        sliced = ctx.enter_context(tc.tile_pool(name="sliced", bufs=2))
        turned = ctx.enter_context(tc.tile_pool(name="turned", bufs=2))
        psum = ctx.enter_context(tc.psum_pool(name="psum", bufs=7))
        psum_fold = ctx.enter_context(tc.psum_pool(name="psum_fold", bufs=1))

        x_codes = keep.tile([P, PASSES, IN], U32, align_bytes=64)
        x_scales = keep.tile([P, PASSES, IN], U8, align_bytes=64)
        g_codes = keep.tile([P, PASSES, OUT], U32, align_bytes=64)
        g_scales = keep.tile([P, PASSES, OUT], U8, align_bytes=64)

        warm_in = keep.tile([P, 1], F32)
        warm_out = keep.tile([P, 1], F32)
        nc.vector.memset(warm_in[:], 0.0)
        nc.scalar.activation(out=warm_out[:], in_=warm_in[:], func=ACT.Sigmoid)

        ident = keep.tile([P, P], F32)
        make_identity(nc, ident[:])
        chooser = keep.tile([P, GROUPS], F32)
        nc.vector.tensor_reduce(
            out=chooser[:], in_=ident[:].rearrange("p (k u) -> p k u", u=KEPT), axis=mybir.AxisListType.X, op=ALU.add
        )

        def regroup(engine_copy, raw, first):
            grouped = groupeds.tile([P, HALF, PACK], BF16, align_bytes=64)
            engine_copy(
                out=grouped[:].rearrange("p (r i) j -> p r j i", i=RUN),
                in_=raw[:, :, first : first + HALF].rearrange("p j (r i) -> p r j i", i=RUN),
            )
            return grouped

        def quantise(grouped, codes, scales, fmt, c, first):
            nc.vector.quantize_mx(
                out=codes[:, c, first : first + HALF].bitcast(fmt),
                scales=scales[:, c, first : first + HALF],
                in_=grouped[:].rearrange("p w j -> p (w j)"),
            )

        def prepare(units, first_copy):
            scalars_half = None
            for rows, codes, scales, fmt, c, h in units:
                first = h * UNIT
                raw = raws.tile([P, PACK, UNIT], BF16)
                nc.sync.dma_start(
                    out=raw[:],
                    in_=rows[c * K_PASS : (c + 1) * K_PASS, first : first + UNIT].rearrange(
                        "(p j) w -> p j w", j=PACK
                    ),
                )
                by_vector = regroup(first_copy, raw, 0)
                by_scalar = regroup(nc.scalar.copy, raw, HALF)
                if scalars_half is not None:
                    quantise(*scalars_half)
                quantise(by_vector, codes, scales, fmt, c, first)
                scalars_half = (by_scalar, codes, scales, fmt, c, first + HALF)
            quantise(*scalars_half)

        x_units = [(x_rows, x_codes, x_scales, E4M3X4, c, h) for h in range(IN // UNIT) for c in range(PASSES)]
        g_units = [(g_rows, g_codes, g_scales, E5M2X4, c, h) for h in range(OUT // UNIT) for c in range(PASSES)]
        prepare(x_units[:PASSES] + g_units[:PASSES] + x_units[PASSES:], nc.vector.tensor_copy)

        rs_sb = keep.tile([P, O_TILES, GROUPS], BF16)
        sig = keep.tile([P, O_TILES, GROUPS], F32)
        sums = keep.tile([P, O_TILES, GROUPS], F32)

        def sum_by_tensor(t, slices):
            fold = psum_fold.tile([P, BANK], F32)
            for j in range(SLICES):
                nc.tensor.matmul(
                    out=fold[:, :P],
                    lhsT=slices[:, j, :],
                    rhs=ident[:],
                    is_transpose=True,
                    start=(j == 0),
                    stop=(j == SLICES - 1),
                )
            fold_sb = turned.tile([P, P], F32)
            nc.scalar.copy(out=fold_sb[:], in_=fold[:, :P])
            group_sums = fold[:, P : P + GROUPS]
            nc.tensor.matmul(out=group_sums, lhsT=fold_sb[:], rhs=chooser[:], start=True, stop=True)
            nc.scalar.copy(out=sums[:, t, :], in_=group_sums)

        def store(end):
            done = slice(end - STORE_TILES, end)
            result = stores.tile([P, STORE_TILES, GROUPS], F32)
            nc.vector.scalar_tensor_tensor(
                out=result[:], in0=sums[:, done, :], scalar=2.0, in1=sig[:, done, :], op0=ALU.mult, op1=ALU.mult
            )
            nc.sync.dma_start(out=out_view[:, done, :], in_=result[:])

        late_raws = []
        late_halves = [(c, UNIT + h * HALF) for h in range(UNIT // HALF) for c in range(PASSES)]
        late_grouped = []
        waiting = []
        half_signs = {}
        slices_of = {}

        def start_tile(t):
            if t % TENSOR_EVERY == 1:
                slices = sliced.tile([P, SLICES, P], F32)
                slices_of[t] = slices
            w_sb = weights.tile([P, IN], BF16)
            nc.sync.dma_start(out=w_sb[:], in_=w_tiles[t])
            if t == EARLY_TILES - 1:
                for c in range(PASSES):
                    late_raw = raws.tile([P, PACK, UNIT], BF16, name="raw")
                    nc.sync.dma_start(
                        out=late_raw[:],
                        in_=g_rows[c * K_PASS : (c + 1) * K_PASS, UNIT : 2 * UNIT].rearrange("(p j) w -> p j w", j=PACK),
                    )
                    late_raws.append(late_raw)
            half_sign = signs.tile([P, IN], BF16)
            nc.vector.tensor_scalar(
                out=half_sign[:], in0=w_sb[:], scalar1=0.0, scalar2=0.5, op0=ALU.is_ge, op1=ALU.subtract
            )
            half_signs[t] = half_sign

        def bank(t, b):
            o_cols = slice(t * P, (t + 1) * P)
            i_cols = slice(b * BANK, (b + 1) * BANK)
            half_sign = half_signs[t]
            acc = psum.tile([P, BANK], F32)
            for c in range(PASSES):
                nc.tensor.matmul_mx(
                    out=acc[:],
                    lhsT=g_codes[:, c, o_cols].bitcast(E5M2X4),
                    lhsT_scale=g_scales[:, c, o_cols],
                    rhs=x_codes[:, c, i_cols].bitcast(E4M3X4),
                    rhs_scale=x_scales[:, c, i_cols],
                    start=(c == 0),
                    stop=(c == PASSES - 1),
                )
            if t in slices_of:
                places = slice(b * GROUPS_PER_BANK * KEPT, (b + 1) * GROUPS_PER_BANK * KEPT)
                nc.vector.tensor_tensor(
                    out=slices_of[t][:, :, places].rearrange("p j (k u) -> p j k u", u=KEPT),
                    in0=acc[:].rearrange("p (k j u) -> p j k u", j=SLICES, u=KEPT),
                    in1=half_sign[:, i_cols].rearrange("p (k j u) -> p j k u", j=SLICES, u=KEPT),
                    op=ALU.mult,
                )
                return
            prod = prods.tile([P, BANK], F32)
            if t == O_TILES - 1 and b >= BANKS - BANKS_BY_VECTOR:
                for q in range(GROUPS_PER_BANK):
                    k = b * GROUPS_PER_BANK + q
                    nc.vector.scalar_tensor_tensor(
                        out=prod[:, q * GROUP : (q + 1) * GROUP],
                        in0=acc[:, q * GROUP : (q + 1) * GROUP],
                        scalar=1.0,
                        in1=half_sign[:, k * GROUP : (k + 1) * GROUP],
                        op0=ALU.mult,
                        op1=ALU.mult,
                        accum_out=sums[:, t, k : k + 1],
                    )
                return
            nc.vector.tensor_tensor(out=prod[:], in0=acc[:], in1=half_sign[:, i_cols], op=ALU.mult)
            for q in range(GROUPS_PER_BANK):
                k = b * GROUPS_PER_BANK + q
                group_cols = slice(q * GROUP, (q + 1) * GROUP)
                nc.scalar.activation(
                    out=prod[:, group_cols], in_=prod[:, group_cols], func=ACT.Copy, accum_out=sums[:, t, k : k + 1]
                )

        def end_tile(t):
            if waiting and waiting[0][0] <= t - TENSOR_LAG:
                sum_by_tensor(*waiting.pop())
            if t in slices_of:
                waiting.append((t, slices_of[t]))
            if late_grouped and late_grouped[0][0] <= t - QUANTISE_LAG:
                quantise(*late_grouped.pop(0)[1])
            if t in slices_of and late_halves:
                c, first = late_halves.pop(0)
                late_grouped.append(
                    (
                        min(t, O_TILES - 7),
                        (regroup(nc.scalar.copy, late_raws[c], first - UNIT), g_codes, g_scales, E5M2X4, c, first),
                    )
                )
            if t == LATE_UNITS_AFTER_TILE:
                nc.sync.dma_start(out=rs_sb[:], in_=rs_view)
                nc.scalar.activation(out=sig[:], in_=rs_sb[:], func=ACT.Sigmoid)
            if t % STORE_TILES == STORE_LAG and t > STORE_TILES:
                store(t - STORE_LAG)

        for t in range(EARLY_TILES):
            start_tile(t)
            for b in range(BANKS // 2):
                bank(t, b)
        for t in range(EARLY_TILES):
            for b in range(BANKS // 2, BANKS):
                bank(t, b)
            end_tile(t)
        for t in range(EARLY_TILES, O_TILES):
            start_tile(t)
            for b in range(BANKS):
                bank(t, b)
            end_tile(t)
        store(O_TILES)
